import numpy as np
import ml_dtypes


def mxq(x, axis, fmt="e4m3"):
    dtype, down = {"e4m3": (ml_dtypes.float8_e4m3fn, 7), "e5m2": (ml_dtypes.float8_e5m2, 14)}[fmt]
    v = np.moveaxis(np.asarray(x, np.float32).astype(ml_dtypes.bfloat16).astype(np.float64), axis, -1)
    blocks = v.reshape(v.shape[:-1] + (-1, 32))
    amax = np.abs(blocks).max(-1, keepdims=True)
    byte = np.maximum(np.where(amax > 0, np.frexp(amax)[1] - 1 + 127, 0) - down, 1)
    scale = np.exp2(byte - 127.0)
    codes = (blocks / scale).astype(np.float32).astype(dtype).astype(np.float64)
    return np.moveaxis((codes * scale).reshape(v.shape), -1, axis)


WIDE = False


def mx_kscale(k):
    if not WIDE:
        return np.ones(k)
    levels = np.array([10, -10, 5, -5, 0])
    a = np.random.permutation(np.resize(levels, k // 512 * 4)).reshape(k // 512, 4)
    idx = np.arange(k)
    return np.exp2(a[idx // 512, idx % 128 // 32])


BF16 = ml_dtypes.bfloat16


def bf(x):
    return np.asarray(x, np.float32).astype(BF16)


def f64(x):
    return np.asarray(x).astype(np.float64)


B, T, D, H = 1, 512, 2048, 16
HD = D // H
SCALE = HD ** (-0.5)


def rotate_half(u):
    u1, u2 = np.split(u, 2, axis=-1)
    return np.concatenate([-u2, u1], axis=-1)


def apply_rope(u, sin, cos):
    return u * cos[None, :, None, :] + rotate_half(u) * sin[None, :, None, :]


def setup_inputs():
    s = mx_kscale(D)
    return {"x": bf(np.random.standard_normal((B, T, D)) * s),
            "sin": bf(np.random.standard_normal((T, HD))),
            "cos": bf(np.random.standard_normal((T, HD))),
            "W_qkv": bf(np.random.standard_normal((D, D + 2 * HD)) * 2.0 / np.sqrt(D) / s[:, None])}


def reference(x, sin, cos, W_qkv):
    sin, cos = f64(sin), f64(cos)
    qkv = mxq(f64(x), 2, "e4m3") @ mxq(f64(W_qkv), 0, "e4m3")
    q, k, v = np.split(qkv, [D, D + HD], axis=-1)
    q = q.reshape(B, T, H, HD) * SCALE
    q_rot = np.ascontiguousarray(apply_rope(q, sin, cos).transpose(0, 2, 1, 3))
    k_rot = apply_rope(k[:, :, None, :], sin, cos)[:, :, 0, :]
    return q_rot, k_rot, v

@@ -1,0 +1,231 @@
+from contextlib import ExitStack
+
+import concourse.mybir as mybir
+from concourse.masks import make_identity
+
+F32 = mybir.dt.float32
+BF16 = mybir.dt.bfloat16
+U32 = mybir.dt.uint32
+U8 = mybir.dt.uint8
+FP8X4 = mybir.dt.float8_e4m3fn_x4
+MULT = mybir.AluOpType.mult
+ADD = mybir.AluOpType.add
+
+P = 128
+PACK = 4
+K_PASS = P * PACK
+TOKENS = 512
+D_MODEL = 2048
+HEAD_DIM = 128
+HALF = HEAD_DIM // 2
+Q_HEADS = 16
+N_COLS = (Q_HEADS + 2) * HEAD_DIM
+PASSES = D_MODEL // K_PASS
+TOKEN_BLOCKS = TOKENS // P
+GROUP_COLS = 512
+Q_SCALE = HEAD_DIM**-0.5
+RUN = 4
+
+FLOPS = 2 * TOKENS * D_MODEL * N_COLS
+
+
+def tile_multiqueryattention_pa_kernel(tc, x, sin, cos, W_qkv, out_0, out_1, out_2):
+    nc = tc.nc
+    groups = [(first, min(GROUP_COLS, N_COLS - first)) for first in range(0, N_COLS, GROUP_COLS)]
+    assert PASSES == TOKEN_BLOCKS
+
+    x_blocks = x.rearrange("b (m r) k -> (b m) r k", r=TOKEN_BLOCKS)
+    cos_blocks = cos.rearrange("(m r) d -> m r d", r=TOKEN_BLOCKS)
+    sin_blocks = sin.rearrange("(m r) d -> m r d", r=TOKEN_BLOCKS)
+    q_view = out_0.rearrange("b h (m r) d -> m (b h) (r d)", r=TOKEN_BLOCKS)
+    k_view = out_1.rearrange("b (m r) d -> m b (r d)", r=TOKEN_BLOCKS)
+    v_view = out_2.rearrange("b (m r) d -> m b (r d)", r=TOKEN_BLOCKS)
+
+    with ExitStack() as ctx:
+        const = ctx.enter_context(tc.tile_pool(name="const", bufs=1))
+        x_pool = ctx.enter_context(tc.tile_pool(name="x_pool", bufs=TOKEN_BLOCKS))
+        x_stage = ctx.enter_context(tc.tile_pool(name="x_stage", bufs=2))
+        raw_pool = ctx.enter_context(tc.tile_pool(name="raw_pool", bufs=len(groups) * PASSES))
+        grouped_pool = ctx.enter_context(tc.tile_pool(name="grouped_pool", bufs=4))
+        codes_pool = ctx.enter_context(tc.tile_pool(name="codes_pool", bufs=3))
+        out_pool = ctx.enter_context(tc.tile_pool(name="out_pool", bufs=3))
+        psum = ctx.enter_context(tc.psum_pool(name="psum", bufs=8))
+        ctx.enter_context(tc.manual_schedule())
+
+        def load_x_block(r):
+            x_rows = x_pool.tile([P, D_MODEL], BF16)
+            nc.sync.dma_start(out=x_rows[:], in_=x_blocks[:, r, :])
+            return x_rows
+
+        def load_w_chunk(g, c):
+            first, width = groups[g]
+            w_raw = raw_pool.tile([P, PACK, width], BF16)
+            for u in range(2):
+                row = K_PASS * c + 2 * P * u
+                nc.sync.dma_start(
+                    out=w_raw[:, 2 * u : 2 * u + 2, :],
+                    in_=W_qkv[row : row + 2 * P, first : first + width].rearrange(
+                        "(p e) w -> p e w", e=2
+                    ),
+                )
+            return w_raw
+
+        cos_raw = const.tile([P, TOKEN_BLOCKS, HEAD_DIM], BF16)
+        sin_raw = const.tile([P, TOKEN_BLOCKS, HEAD_DIM], BF16)
+        nc.scalar.dma_start(out=cos_raw[:], in_=cos_blocks)
+        nc.scalar.dma_start(out=sin_raw[:], in_=sin_blocks)
+
+        w_raw_of = {}
+        x_rows_of = []
+        for i in range(PASSES):
+            w_raw_of[(0, i)] = load_w_chunk(0, i)
+            x_rows_of.append(load_x_block(i))
+        for g in range(1, len(groups)):
+            for c in range(PASSES):
+                w_raw_of[(g, c)] = load_w_chunk(g, c)
+
+        identity = const.tile([P, P], F32)
+        make_identity(nc, identity[:])
+
+        def make_tables(factor, cos_table, sin_table):
+            nc.gpsimd.tensor_scalar(
+                out=cos_table[:], in0=cos_raw[:], scalar1=factor, scalar2=0.0, op0=MULT, op1=ADD
+            )
+            nc.gpsimd.tensor_scalar(
+                out=sin_table[:, :, 0:HALF], in0=sin_raw[:, :, 0:HALF],
+                scalar1=-factor, scalar2=0.0, op0=MULT, op1=ADD,
+            )
+            nc.gpsimd.tensor_scalar(
+                out=sin_table[:, :, HALF:HEAD_DIM], in0=sin_raw[:, :, HALF:HEAD_DIM],
+                scalar1=factor, scalar2=0.0, op0=MULT, op1=ADD,
+            )
+
+        cos_q = const.tile([P, TOKEN_BLOCKS, HEAD_DIM], F32)
+        sin_q = const.tile([P, TOKEN_BLOCKS, HEAD_DIM], F32)
+        cos_k = const.tile([P, TOKEN_BLOCKS, HEAD_DIM], F32)
+        sin_k = const.tile([P, TOKEN_BLOCKS, HEAD_DIM], F32)
+        make_tables(Q_SCALE, cos_q, sin_q)
+        make_tables(1.0, cos_k, sin_k)
+
+        x_codes = const.tile([P, TOKEN_BLOCKS, PASSES * P], U32, align_bytes=64)
+        x_scales = const.tile([P, TOKEN_BLOCKS, PASSES * P], U8, align_bytes=64)
+
+        def transpose_x_block(r):
+            x_words = x_rows_of[r][:].bitcast(F32)
+            x_grouped = x_stage.tile([P, PASSES * P * PACK], BF16, align_bytes=64)
+            grouped_words = x_grouped[:].bitcast(F32).rearrange("p (n u) -> p n u", u=2)
+            for b in range(PASSES // 2):
+                bank = psum.tile([P, GROUP_COLS], F32, tag="bank")
+                for u in range(2):
+                    for cc in range(2):
+                        word = 2 * P * (2 * b + cc) + P * u
+                        nc.tensor.transpose(
+                            bank[:, (2 * u + cc) * P : (2 * u + cc + 1) * P],
+                            x_words[:, word : word + P],
+                            identity[:],
+                        )
+                nc.vector.tensor_copy(
+                    out=grouped_words[:, 2 * P * b : 2 * P * (b + 1), :],
+                    in_=bank[:].rearrange("p (u n) -> p n u", u=2),
+                )
+            return x_grouped
+
+        def quantise_x_block(r, x_grouped):
+            nc.vector.quantize_mx(
+                out=x_codes[:, r, :].bitcast(FP8X4), scales=x_scales[:, r, :], in_=x_grouped[:]
+            )
+
+        def regroup_w_chunk(g, c):
+            width = groups[g][1]
+            w_grouped = grouped_pool.tile([P, width, PACK], BF16, align_bytes=64)
+            nc.scalar.copy(
+                out=w_grouped[:].rearrange("p (n i) t -> p n t i", i=RUN),
+                in_=w_raw_of[(g, c)][:].rearrange("p t (n i) -> p n t i", i=RUN),
+            )
+            return w_grouped
+
+        def quantise_w_chunk(g, c, w_grouped, w_codes, w_scales):
+            width = groups[g][1]
+            nc.vector.quantize_mx(
+                out=w_codes[:, c, 0:width].bitcast(FP8X4),
+                scales=w_scales[:, c, 0:width],
+                in_=w_grouped[:].rearrange("p n t -> p (n t)"),
+            )
+
+        def new_w_operand():
+            w_codes = codes_pool.tile([P, PASSES, GROUP_COLS], U32, align_bytes=64)
+            w_scales = codes_pool.tile([P, PASSES, GROUP_COLS], U8, align_bytes=64)
+            return w_codes, w_scales
+
+        def multiply(g, r, w_codes, w_scales):
+            width = groups[g][1]
+            bank = psum.tile([P, GROUP_COLS], F32, tag="bank")
+            for c in range(PASSES):
+                nc.tensor.matmul_mx(
+                    out=bank[:, 0:width],
+                    lhsT=x_codes[:, r, c * P : (c + 1) * P].bitcast(FP8X4),
+                    lhsT_scale=x_scales[:, r, c * P : (c + 1) * P],
+                    rhs=w_codes[:, c, 0:width].bitcast(FP8X4),
+                    rhs_scale=w_scales[:, c, 0:width],
+                    start=(c == 0),
+                    stop=(c == PASSES - 1),
+                )
+            return bank
+
+        def rope(heads, u, cos_table, sin_table, direct, crossed):
+            nc.vector.tensor_tensor(
+                out=direct, in0=u,
+                in1=cos_table.unsqueeze(1).to_broadcast([P, heads, HEAD_DIM]), op=MULT,
+            )
+            for half in range(2):
+                here = slice(half * HALF, (half + 1) * HALF)
+                other = slice((1 - half) * HALF, (2 - half) * HALF)
+                nc.vector.tensor_tensor(
+                    out=crossed[:, :, here], in0=u[:, :, other],
+                    in1=sin_table[:, here].unsqueeze(1).to_broadcast([P, heads, HALF]), op=MULT,
+                )
+            nc.gpsimd.tensor_tensor(out=direct, in0=direct, in1=crossed, op=ADD)
+
+        operand = new_w_operand()
+        for i in range(PASSES):
+            w_grouped = regroup_w_chunk(0, i)
+            x_grouped = transpose_x_block(i)
+            quantise_w_chunk(0, i, w_grouped, operand[0], operand[1])
+            quantise_x_block(i, x_grouped)
+
+        for g in range(len(groups)):
+            first, width = groups[g]
+            is_q = first < Q_HEADS * HEAD_DIM
+            heads = width // HEAD_DIM if is_q else 1
+            direct = out_pool.tile([P, heads, TOKEN_BLOCKS, HEAD_DIM], F32, tag="direct")
+            crossed = out_pool.tile([P, heads, TOKEN_BLOCKS, HEAD_DIM], F32, tag="crossed")
+            if not is_q:
+                v_rows = out_pool.tile([P, 1, TOKEN_BLOCKS, HEAD_DIM], F32, tag="v_rows")
+            if g + 1 < len(groups):
+                next_operand = new_w_operand()
+            for i in range(TOKEN_BLOCKS):
+                if g + 1 < len(groups):
+                    w_grouped = regroup_w_chunk(g + 1, i)
+                    quantise_w_chunk(g + 1, i, w_grouped, next_operand[0], next_operand[1])
+                bank = multiply(g, i, operand[0], operand[1])
+                rope(
+                    heads,
+                    bank[:, 0 : heads * HEAD_DIM].rearrange("p (h d) -> p h d", d=HEAD_DIM),
+                    (cos_q if is_q else cos_k)[:, i, :],
+                    (sin_q if is_q else sin_k)[:, i, :],
+                    direct[:, :, i, :],
+                    crossed[:, :, i, :],
+                )
+                if not is_q:
+                    nc.vector.tensor_copy(out=v_rows[:, 0, i, :], in_=bank[:, HEAD_DIM : 2 * HEAD_DIM])
+            if is_q:
+                head = first // HEAD_DIM
+                nc.gpsimd.dma_start(
+                    out=q_view[:, head : head + heads, :],
+                    in_=direct[:].rearrange("p h r d -> p h (r d)"),
+                )
+            else:
+                nc.sync.dma_start(out=v_view, in_=v_rows[:].rearrange("p h r d -> p h (r d)"))
+                nc.gpsimd.dma_start(out=k_view, in_=direct[:].rearrange("p h r d -> p h (r d)"))
+            if g + 1 < len(groups):
+                operand = next_operand

@@ -184,7 +184,6 @@ def tile_multiqueryattention_pa_kernel(tc, x, sin, cos, W_qkv, out_0, out_1, out
                     out=crossed[:, :, here], in0=u[:, :, other],
                     in1=sin_table[:, here].unsqueeze(1).to_broadcast([P, heads, HALF]), op=MULT,
                 )
-            nc.gpsimd.tensor_tensor(out=direct, in0=direct, in1=crossed, op=ADD)
 
         operand = new_w_operand()
         for i in range(PASSES):
@@ -218,6 +217,7 @@ def tile_multiqueryattention_pa_kernel(tc, x, sin, cos, W_qkv, out_0, out_1, out
                 )
                 if not is_q:
                     nc.vector.tensor_copy(out=v_rows[:, 0, i, :], in_=bank[:, HEAD_DIM : 2 * HEAD_DIM])
+            nc.vector.tensor_tensor(out=direct[:], in0=direct[:], in1=crossed[:], op=ADD)
             if is_q:
                 head = first // HEAD_DIM
                 nc.gpsimd.dma_start(

@@ -25,6 +25,8 @@ TOKEN_BLOCKS = TOKENS // P
 GROUP_COLS = 512
 Q_SCALE = HEAD_DIM**-0.5
 RUN = 4
+X_AHEAD = 2
+VECTOR_SHARE = 8
 
 FLOPS = 2 * TOKENS * D_MODEL * N_COLS
 
@@ -32,7 +34,6 @@ FLOPS = 2 * TOKENS * D_MODEL * N_COLS
 def tile_multiqueryattention_pa_kernel(tc, x, sin, cos, W_qkv, out_0, out_1, out_2):
     nc = tc.nc
     groups = [(first, min(GROUP_COLS, N_COLS - first)) for first in range(0, N_COLS, GROUP_COLS)]
-    assert PASSES == TOKEN_BLOCKS
 
     x_blocks = x.rearrange("b (m r) k -> (b m) r k", r=TOKEN_BLOCKS)
     cos_blocks = cos.rearrange("(m r) d -> m r d", r=TOKEN_BLOCKS)
@@ -43,18 +44,22 @@ def tile_multiqueryattention_pa_kernel(tc, x, sin, cos, W_qkv, out_0, out_1, out
 
     with ExitStack() as ctx:
         const = ctx.enter_context(tc.tile_pool(name="const", bufs=1))
-        x_pool = ctx.enter_context(tc.tile_pool(name="x_pool", bufs=TOKEN_BLOCKS))
-        x_stage = ctx.enter_context(tc.tile_pool(name="x_stage", bufs=2))
+        x_pool = ctx.enter_context(tc.tile_pool(name="x_pool", bufs=PASSES))
+        x_stage = ctx.enter_context(tc.tile_pool(name="x_stage", bufs=X_AHEAD + 1))
         raw_pool = ctx.enter_context(tc.tile_pool(name="raw_pool", bufs=len(groups) * PASSES))
         grouped_pool = ctx.enter_context(tc.tile_pool(name="grouped_pool", bufs=4))
         codes_pool = ctx.enter_context(tc.tile_pool(name="codes_pool", bufs=3))
+        product_pool = ctx.enter_context(tc.tile_pool(name="product_pool", bufs=4))
         out_pool = ctx.enter_context(tc.tile_pool(name="out_pool", bufs=3))
         psum = ctx.enter_context(tc.psum_pool(name="psum", bufs=8))
         ctx.enter_context(tc.manual_schedule())
 
-        def load_x_block(r):
-            x_rows = x_pool.tile([P, D_MODEL], BF16)
-            nc.sync.dma_start(out=x_rows[:], in_=x_blocks[:, r, :])
+        def load_x_chunk(c):
+            x_rows = x_pool.tile([P, TOKEN_BLOCKS * K_PASS], BF16)
+            nc.sync.dma_start(
+                out=x_rows[:].rearrange("p (r k) -> p r k", r=TOKEN_BLOCKS),
+                in_=x_blocks[:, :, c * K_PASS : (c + 1) * K_PASS],
+            )
             return x_rows
 
         def load_w_chunk(g, c):
@@ -77,9 +82,9 @@ def tile_multiqueryattention_pa_kernel(tc, x, sin, cos, W_qkv, out_0, out_1, out
 
         w_raw_of = {}
         x_rows_of = []
-        for i in range(PASSES):
-            w_raw_of[(0, i)] = load_w_chunk(0, i)
-            x_rows_of.append(load_x_block(i))
+        for c in range(PASSES):
+            w_raw_of[(0, c)] = load_w_chunk(0, c)
+            x_rows_of.append(load_x_chunk(c))
         for g in range(1, len(groups)):
             for c in range(PASSES):
                 w_raw_of[(g, c)] = load_w_chunk(g, c)
@@ -107,40 +112,52 @@ def tile_multiqueryattention_pa_kernel(tc, x, sin, cos, W_qkv, out_0, out_1, out
         make_tables(Q_SCALE, cos_q, sin_q)
         make_tables(1.0, cos_k, sin_k)
 
-        x_codes = const.tile([P, TOKEN_BLOCKS, PASSES * P], U32, align_bytes=64)
-        x_scales = const.tile([P, TOKEN_BLOCKS, PASSES * P], U8, align_bytes=64)
+        x_codes = const.tile([P, PASSES, TOKENS], U32, align_bytes=64)
+        x_scales = const.tile([P, PASSES, TOKENS], U8, align_bytes=64)
 
-        def transpose_x_block(r):
-            x_words = x_rows_of[r][:].bitcast(F32)
-            x_grouped = x_stage.tile([P, PASSES * P * PACK], BF16, align_bytes=64)
-            grouped_words = x_grouped[:].bitcast(F32).rearrange("p (n u) -> p n u", u=2)
-            for b in range(PASSES // 2):
+        def transpose_x_chunk(c):
+            x_words = x_rows_of[c][:].bitcast(F32)
+            x_banks = []
+            for b in range(TOKEN_BLOCKS // 2):
                 bank = psum.tile([P, GROUP_COLS], F32, tag="bank")
                 for u in range(2):
-                    for cc in range(2):
-                        word = 2 * P * (2 * b + cc) + P * u
+                    for rr in range(2):
+                        word = 2 * P * (2 * b + rr) + P * u
                         nc.tensor.transpose(
-                            bank[:, (2 * u + cc) * P : (2 * u + cc + 1) * P],
+                            bank[:, (2 * u + rr) * P : (2 * u + rr + 1) * P],
                             x_words[:, word : word + P],
                             identity[:],
                         )
+                x_banks.append(bank)
+            return x_banks
+
+        def collect_x_chunk(x_banks):
+            x_grouped = x_stage.tile([P, TOKENS * PACK], BF16, align_bytes=64)
+            grouped_words = x_grouped[:].bitcast(F32).rearrange("p (n u) -> p n u", u=2)
+            for b in range(TOKEN_BLOCKS // 2):
                 nc.vector.tensor_copy(
                     out=grouped_words[:, 2 * P * b : 2 * P * (b + 1), :],
-                    in_=bank[:].rearrange("p (u n) -> p n u", u=2),
+                    in_=x_banks[b][:].rearrange("p (u n) -> p n u", u=2),
                 )
             return x_grouped
 
-        def quantise_x_block(r, x_grouped):
+        def quantise_x_chunk(c, x_grouped):
             nc.vector.quantize_mx(
-                out=x_codes[:, r, :].bitcast(FP8X4), scales=x_scales[:, r, :], in_=x_grouped[:]
+                out=x_codes[:, c, :].bitcast(FP8X4), scales=x_scales[:, c, :], in_=x_grouped[:]
             )
 
         def regroup_w_chunk(g, c):
             width = groups[g][1]
+            split = width - width // VECTOR_SHARE
             w_grouped = grouped_pool.tile([P, width, PACK], BF16, align_bytes=64)
+            w_raw = w_raw_of[(g, c)]
             nc.scalar.copy(
-                out=w_grouped[:].rearrange("p (n i) t -> p n t i", i=RUN),
-                in_=w_raw_of[(g, c)][:].rearrange("p t (n i) -> p n t i", i=RUN),
+                out=w_grouped[:, 0:split, :].rearrange("p (n i) t -> p n t i", i=RUN),
+                in_=w_raw[:, :, 0:split].rearrange("p t (n i) -> p n t i", i=RUN),
+            )
+            nc.vector.tensor_copy(
+                out=w_grouped[:, split:width, :].rearrange("p (n i) t -> p n t i", i=RUN),
+                in_=w_raw[:, :, split:width].rearrange("p t (n i) -> p n t i", i=RUN),
             )
             return w_grouped
 
@@ -152,29 +169,33 @@ def tile_multiqueryattention_pa_kernel(tc, x, sin, cos, W_qkv, out_0, out_1, out
                 in_=w_grouped[:].rearrange("p n t -> p (n t)"),
             )
 
-        def new_w_operand():
+        def open_group():
             w_codes = codes_pool.tile([P, PASSES, GROUP_COLS], U32, align_bytes=64)
             w_scales = codes_pool.tile([P, PASSES, GROUP_COLS], U8, align_bytes=64)
-            return w_codes, w_scales
+            banks = [
+                psum.tile([P, GROUP_COLS], F32, tag="bank", name="acc")
+                for r in range(TOKEN_BLOCKS)
+            ]
+            return w_codes, w_scales, banks
 
-        def multiply(g, r, w_codes, w_scales):
+        def multiply_chunk(g, c, w_codes, w_scales, banks):
             width = groups[g][1]
-            bank = psum.tile([P, GROUP_COLS], F32, tag="bank")
-            for c in range(PASSES):
+            for r in range(TOKEN_BLOCKS):
                 nc.tensor.matmul_mx(
-                    out=bank[:, 0:width],
-                    lhsT=x_codes[:, r, c * P : (c + 1) * P].bitcast(FP8X4),
-                    lhsT_scale=x_scales[:, r, c * P : (c + 1) * P],
+                    out=banks[r][:, 0:width],
+                    lhsT=x_codes[:, c, r * P : (r + 1) * P].bitcast(FP8X4),
+                    lhsT_scale=x_scales[:, c, r * P : (r + 1) * P],
                     rhs=w_codes[:, c, 0:width].bitcast(FP8X4),
                     rhs_scale=w_scales[:, c, 0:width],
                     start=(c == 0),
                     stop=(c == PASSES - 1),
                 )
-            return bank
 
-        def rope(heads, u, cos_table, sin_table, direct, crossed):
+        def rope(heads, u, cos_table, sin_table, rotated):
+            direct = product_pool.tile([P, heads, HEAD_DIM], F32)
+            crossed = product_pool.tile([P, heads, HEAD_DIM], F32)
             nc.vector.tensor_tensor(
-                out=direct, in0=u,
+                out=direct[:], in0=u,
                 in1=cos_table.unsqueeze(1).to_broadcast([P, heads, HEAD_DIM]), op=MULT,
             )
             for half in range(2):
@@ -184,48 +205,65 @@ def tile_multiqueryattention_pa_kernel(tc, x, sin, cos, W_qkv, out_0, out_1, out
                     out=crossed[:, :, here], in0=u[:, :, other],
                     in1=sin_table[:, here].unsqueeze(1).to_broadcast([P, heads, HALF]), op=MULT,
                 )
+            nc.gpsimd.tensor_tensor(out=rotated, in0=direct[:], in1=crossed[:], op=ADD)
 
-        operand = new_w_operand()
-        for i in range(PASSES):
-            w_grouped = regroup_w_chunk(0, i)
-            x_grouped = transpose_x_block(i)
-            quantise_w_chunk(0, i, w_grouped, operand[0], operand[1])
-            quantise_x_block(i, x_grouped)
+        def finish_bank(g, r, bank, rotated, v_rows):
+            first, width = groups[g]
+            is_q = first < Q_HEADS * HEAD_DIM
+            heads = rotated.shape[1]
+            rope(
+                heads,
+                bank[:, 0 : heads * HEAD_DIM].rearrange("p (h d) -> p h d", d=HEAD_DIM),
+                (cos_q if is_q else cos_k)[:, r, :],
+                (sin_q if is_q else sin_k)[:, r, :],
+                rotated[:, :, r, :],
+            )
+            if not is_q:
+                nc.vector.tensor_copy(out=v_rows[:, 0, r, :], in_=bank[:, HEAD_DIM : 2 * HEAD_DIM])
+            if r == TOKEN_BLOCKS - 1:
+                if is_q:
+                    head = first // HEAD_DIM
+                    nc.sync.dma_start(
+                        out=q_view[:, head : head + heads, :],
+                        in_=rotated[:].rearrange("p h r d -> p h (r d)"),
+                    )
+                else:
+                    nc.sync.dma_start(out=v_view, in_=v_rows[:].rearrange("p h r d -> p h (r d)"))
+                    nc.sync.dma_start(out=k_view, in_=rotated[:].rearrange("p h r d -> p h (r d)"))
 
-        for g in range(len(groups)):
+        def open_outputs(g):
             first, width = groups[g]
             is_q = first < Q_HEADS * HEAD_DIM
             heads = width // HEAD_DIM if is_q else 1
-            direct = out_pool.tile([P, heads, TOKEN_BLOCKS, HEAD_DIM], F32, tag="direct")
-            crossed = out_pool.tile([P, heads, TOKEN_BLOCKS, HEAD_DIM], F32, tag="crossed")
+            rotated = out_pool.tile([P, heads, TOKEN_BLOCKS, HEAD_DIM], F32, tag="rotated")
+            v_rows = None
             if not is_q:
                 v_rows = out_pool.tile([P, 1, TOKEN_BLOCKS, HEAD_DIM], F32, tag="v_rows")
-            if g + 1 < len(groups):
-                next_operand = new_w_operand()
-            for i in range(TOKEN_BLOCKS):
-                if g + 1 < len(groups):
-                    w_grouped = regroup_w_chunk(g + 1, i)
-                    quantise_w_chunk(g + 1, i, w_grouped, next_operand[0], next_operand[1])
-                bank = multiply(g, i, operand[0], operand[1])
-                rope(
-                    heads,
-                    bank[:, 0 : heads * HEAD_DIM].rearrange("p (h d) -> p h d", d=HEAD_DIM),
-                    (cos_q if is_q else cos_k)[:, i, :],
-                    (sin_q if is_q else sin_k)[:, i, :],
-                    direct[:, :, i, :],
-                    crossed[:, :, i, :],
-                )
-                if not is_q:
-                    nc.vector.tensor_copy(out=v_rows[:, 0, i, :], in_=bank[:, HEAD_DIM : 2 * HEAD_DIM])
-            nc.vector.tensor_tensor(out=direct[:], in0=direct[:], in1=crossed[:], op=ADD)
-            if is_q:
-                head = first // HEAD_DIM
-                nc.gpsimd.dma_start(
-                    out=q_view[:, head : head + heads, :],
-                    in_=direct[:].rearrange("p h r d -> p h (r d)"),
-                )
-            else:
-                nc.sync.dma_start(out=v_view, in_=v_rows[:].rearrange("p h r d -> p h (r d)"))
-                nc.gpsimd.dma_start(out=k_view, in_=direct[:].rearrange("p h r d -> p h (r d)"))
-            if g + 1 < len(groups):
-                operand = next_operand
+            return rotated, v_rows
+
+        assert PASSES == TOKEN_BLOCKS
+        steps = len(groups) * PASSES
+        x_banks_of = [transpose_x_chunk(c) for c in range(PASSES)]
+        w_grouped_next = regroup_w_chunk(0, 0)
+        x_grouped_of = [collect_x_chunk(x_banks_of[c]) for c in range(X_AHEAD)]
+        for n in range(steps):
+            g, c = divmod(n, PASSES)
+            w_grouped = w_grouped_next
+            if n + 1 < steps:
+                w_grouped_next = regroup_w_chunk((n + 1) // PASSES, (n + 1) % PASSES)
+            if c == 0:
+                if g > 0:
+                    done_banks = banks
+                    rotated, v_rows = open_outputs(g - 1)
+                w_codes, w_scales, banks = open_group()
+            quantise_w_chunk(g, c, w_grouped, w_codes, w_scales)
+            if g == 0:
+                quantise_x_chunk(c, x_grouped_of[c])
+            multiply_chunk(g, c, w_codes, w_scales, banks)
+            if g == 0 and c + X_AHEAD < PASSES:
+                x_grouped_of.append(collect_x_chunk(x_banks_of[c + X_AHEAD]))
+            if g > 0:
+                finish_bank(g - 1, c, done_banks[c], rotated, v_rows)
+        rotated, v_rows = open_outputs(len(groups) - 1)
+        for r in range(TOKEN_BLOCKS):
+            finish_bank(len(groups) - 1, r, banks[r], rotated, v_rows)

@@ -26,7 +26,9 @@ GROUP_COLS = 512
 Q_SCALE = HEAD_DIM**-0.5
 RUN = 4
 X_AHEAD = 2
-VECTOR_SHARE = 8
+PSUM_BANKS = 8
+VECTOR_EIGHTHS_FIRST = 3
+VECTOR_EIGHTHS = 1
 
 FLOPS = 2 * TOKENS * D_MODEL * N_COLS
 
@@ -45,21 +47,25 @@ def tile_multiqueryattention_pa_kernel(tc, x, sin, cos, W_qkv, out_0, out_1, out
     with ExitStack() as ctx:
         const = ctx.enter_context(tc.tile_pool(name="const", bufs=1))
         x_pool = ctx.enter_context(tc.tile_pool(name="x_pool", bufs=PASSES))
-        x_stage = ctx.enter_context(tc.tile_pool(name="x_stage", bufs=X_AHEAD + 1))
+        x_stage = ctx.enter_context(tc.tile_pool(name="x_stage", bufs=2))
         raw_pool = ctx.enter_context(tc.tile_pool(name="raw_pool", bufs=len(groups) * PASSES))
         grouped_pool = ctx.enter_context(tc.tile_pool(name="grouped_pool", bufs=4))
         codes_pool = ctx.enter_context(tc.tile_pool(name="codes_pool", bufs=3))
         product_pool = ctx.enter_context(tc.tile_pool(name="product_pool", bufs=4))
         out_pool = ctx.enter_context(tc.tile_pool(name="out_pool", bufs=3))
-        psum = ctx.enter_context(tc.psum_pool(name="psum", bufs=8))
+        psum_even = ctx.enter_context(tc.psum_pool(name="psum_even", bufs=PSUM_BANKS // 2))
+        psum_odd = ctx.enter_context(tc.psum_pool(name="psum_odd", bufs=PSUM_BANKS // 2))
         ctx.enter_context(tc.manual_schedule())
 
         def load_x_chunk(c):
             x_rows = x_pool.tile([P, TOKEN_BLOCKS * K_PASS], BF16)
-            nc.sync.dma_start(
-                out=x_rows[:].rearrange("p (r k) -> p r k", r=TOKEN_BLOCKS),
-                in_=x_blocks[:, :, c * K_PASS : (c + 1) * K_PASS],
-            )
+            for b in range(TOKEN_BLOCKS // 2):
+                nc.sync.dma_start(
+                    out=x_rows[:, 2 * b * K_PASS : (2 * b + 2) * K_PASS].rearrange(
+                        "p (r k) -> p r k", r=2
+                    ),
+                    in_=x_blocks[:, 2 * b : 2 * b + 2, c * K_PASS : (c + 1) * K_PASS],
+                )
             return x_rows
 
         def load_w_chunk(g, c):
@@ -77,14 +83,14 @@ def tile_multiqueryattention_pa_kernel(tc, x, sin, cos, W_qkv, out_0, out_1, out
 
         cos_raw = const.tile([P, TOKEN_BLOCKS, HEAD_DIM], BF16)
         sin_raw = const.tile([P, TOKEN_BLOCKS, HEAD_DIM], BF16)
-        nc.scalar.dma_start(out=cos_raw[:], in_=cos_blocks)
-        nc.scalar.dma_start(out=sin_raw[:], in_=sin_blocks)
 
         w_raw_of = {}
         x_rows_of = []
         for c in range(PASSES):
             w_raw_of[(0, c)] = load_w_chunk(0, c)
             x_rows_of.append(load_x_chunk(c))
+        nc.sync.dma_start(out=cos_raw[:], in_=cos_blocks)
+        nc.sync.dma_start(out=sin_raw[:], in_=sin_blocks)
         for g in range(1, len(groups)):
             for c in range(PASSES):
                 w_raw_of[(g, c)] = load_w_chunk(g, c)
@@ -119,7 +125,7 @@ def tile_multiqueryattention_pa_kernel(tc, x, sin, cos, W_qkv, out_0, out_1, out
             x_words = x_rows_of[c][:].bitcast(F32)
             x_banks = []
             for b in range(TOKEN_BLOCKS // 2):
-                bank = psum.tile([P, GROUP_COLS], F32, tag="bank")
+                bank = psum_odd.tile([P, GROUP_COLS], F32, tag="bank")
                 for u in range(2):
                     for rr in range(2):
                         word = 2 * P * (2 * b + rr) + P * u
@@ -134,11 +140,14 @@ def tile_multiqueryattention_pa_kernel(tc, x, sin, cos, W_qkv, out_0, out_1, out
         def collect_x_chunk(x_banks):
             x_grouped = x_stage.tile([P, TOKENS * PACK], BF16, align_bytes=64)
             grouped_words = x_grouped[:].bitcast(F32).rearrange("p (n u) -> p n u", u=2)
-            for b in range(TOKEN_BLOCKS // 2):
-                nc.vector.tensor_copy(
-                    out=grouped_words[:, 2 * P * b : 2 * P * (b + 1), :],
-                    in_=x_banks[b][:].rearrange("p (u n) -> p n u", u=2),
-                )
+            nc.vector.tensor_copy(
+                out=grouped_words[:, 0 : 2 * P, :],
+                in_=x_banks[0][:].rearrange("p (u n) -> p n u", u=2),
+            )
+            nc.scalar.copy(
+                out=grouped_words[:, 2 * P : 4 * P, :],
+                in_=x_banks[1][:].rearrange("p (u n) -> p n u", u=2),
+            )
             return x_grouped
 
         def quantise_x_chunk(c, x_grouped):
@@ -146,9 +155,9 @@ def tile_multiqueryattention_pa_kernel(tc, x, sin, cos, W_qkv, out_0, out_1, out
                 out=x_codes[:, c, :].bitcast(FP8X4), scales=x_scales[:, c, :], in_=x_grouped[:]
             )
 
-        def regroup_w_chunk(g, c):
+        def regroup_w_chunk(g, c, vector_eighths):
             width = groups[g][1]
-            split = width - width // VECTOR_SHARE
+            split = width - width * vector_eighths // 8
             w_grouped = grouped_pool.tile([P, width, PACK], BF16, align_bytes=64)
             w_raw = w_raw_of[(g, c)]
             nc.scalar.copy(
@@ -169,11 +178,12 @@ def tile_multiqueryattention_pa_kernel(tc, x, sin, cos, W_qkv, out_0, out_1, out
                 in_=w_grouped[:].rearrange("p n t -> p (n t)"),
             )
 
-        def open_group():
+        def open_group(g):
             w_codes = codes_pool.tile([P, PASSES, GROUP_COLS], U32, align_bytes=64)
             w_scales = codes_pool.tile([P, PASSES, GROUP_COLS], U8, align_bytes=64)
+            psum_half = psum_even if g % 2 == 0 else psum_odd
             banks = [
-                psum.tile([P, GROUP_COLS], F32, tag="bank", name="acc")
+                psum_half.tile([P, GROUP_COLS], F32, tag="bank", name="acc")
                 for r in range(TOKEN_BLOCKS)
             ]
             return w_codes, w_scales, banks
@@ -243,25 +253,30 @@ def tile_multiqueryattention_pa_kernel(tc, x, sin, cos, W_qkv, out_0, out_1, out
 
         assert PASSES == TOKEN_BLOCKS
         steps = len(groups) * PASSES
-        x_banks_of = [transpose_x_chunk(c) for c in range(PASSES)]
-        w_grouped_next = regroup_w_chunk(0, 0)
-        x_grouped_of = [collect_x_chunk(x_banks_of[c]) for c in range(X_AHEAD)]
+        x_banks_of = [transpose_x_chunk(c) for c in range(X_AHEAD)]
+        w_grouped_next = regroup_w_chunk(0, 0, VECTOR_EIGHTHS_FIRST)
         for n in range(steps):
             g, c = divmod(n, PASSES)
             w_grouped = w_grouped_next
-            if n + 1 < steps:
-                w_grouped_next = regroup_w_chunk((n + 1) // PASSES, (n + 1) % PASSES)
+            if g == 0:
+                x_grouped = collect_x_chunk(x_banks_of[c])
             if c == 0:
                 if g > 0:
                     done_banks = banks
                     rotated, v_rows = open_outputs(g - 1)
-                w_codes, w_scales, banks = open_group()
+                w_codes, w_scales, banks = open_group(g)
             quantise_w_chunk(g, c, w_grouped, w_codes, w_scales)
             if g == 0:
-                quantise_x_chunk(c, x_grouped_of[c])
+                quantise_x_chunk(c, x_grouped)
             multiply_chunk(g, c, w_codes, w_scales, banks)
+            if n + 1 < steps:
+                w_grouped_next = regroup_w_chunk(
+                    (n + 1) // PASSES,
+                    (n + 1) % PASSES,
+                    VECTOR_EIGHTHS_FIRST if g == 0 else VECTOR_EIGHTHS,
+                )
             if g == 0 and c + X_AHEAD < PASSES:
-                x_grouped_of.append(collect_x_chunk(x_banks_of[c + X_AHEAD]))
+                x_banks_of.append(transpose_x_chunk(c + X_AHEAD))
             if g > 0:
                 finish_bank(g - 1, c, done_banks[c], rotated, v_rows)
         rotated, v_rows = open_outputs(len(groups) - 1)

@@ -25,8 +25,8 @@ TOKEN_BLOCKS = TOKENS // P
 GROUP_COLS = 512
 Q_SCALE = HEAD_DIM**-0.5
 RUN = 4
-X_AHEAD = 2
 PSUM_BANKS = 8
+X_AHEAD = 2
 VECTOR_EIGHTHS_FIRST = 3
 VECTOR_EIGHTHS = 1
 
@@ -36,6 +36,12 @@ FLOPS = 2 * TOKENS * D_MODEL * N_COLS
 def tile_multiqueryattention_pa_kernel(tc, x, sin, cos, W_qkv, out_0, out_1, out_2):
     nc = tc.nc
     groups = [(first, min(GROUP_COLS, N_COLS - first)) for first in range(0, N_COLS, GROUP_COLS)]
+    chunks = [(g, c) for g in range(len(groups)) for c in range(PASSES)]
+    arrivals = []
+    for n in range(len(chunks)):
+        arrivals.append(("w", n))
+        if n < TOKEN_BLOCKS:
+            arrivals.append(("x", n))
 
     x_blocks = x.rearrange("b (m r) k -> (b m) r k", r=TOKEN_BLOCKS)
     cos_blocks = cos.rearrange("(m r) d -> m r d", r=TOKEN_BLOCKS)
@@ -46,9 +52,9 @@ def tile_multiqueryattention_pa_kernel(tc, x, sin, cos, W_qkv, out_0, out_1, out
 
     with ExitStack() as ctx:
         const = ctx.enter_context(tc.tile_pool(name="const", bufs=1))
-        x_pool = ctx.enter_context(tc.tile_pool(name="x_pool", bufs=PASSES))
+        x_pool = ctx.enter_context(tc.tile_pool(name="x_pool", bufs=TOKEN_BLOCKS))
         x_stage = ctx.enter_context(tc.tile_pool(name="x_stage", bufs=2))
-        raw_pool = ctx.enter_context(tc.tile_pool(name="raw_pool", bufs=len(groups) * PASSES))
+        raw_pool = ctx.enter_context(tc.tile_pool(name="raw_pool", bufs=len(chunks)))
         grouped_pool = ctx.enter_context(tc.tile_pool(name="grouped_pool", bufs=4))
         codes_pool = ctx.enter_context(tc.tile_pool(name="codes_pool", bufs=3))
         product_pool = ctx.enter_context(tc.tile_pool(name="product_pool", bufs=4))
@@ -57,15 +63,11 @@ def tile_multiqueryattention_pa_kernel(tc, x, sin, cos, W_qkv, out_0, out_1, out
         psum_odd = ctx.enter_context(tc.psum_pool(name="psum_odd", bufs=PSUM_BANKS // 2))
         ctx.enter_context(tc.manual_schedule())
 
-        def load_x_chunk(c):
-            x_rows = x_pool.tile([P, TOKEN_BLOCKS * K_PASS], BF16)
-            for b in range(TOKEN_BLOCKS // 2):
-                nc.sync.dma_start(
-                    out=x_rows[:, 2 * b * K_PASS : (2 * b + 2) * K_PASS].rearrange(
-                        "p (r k) -> p r k", r=2
-                    ),
-                    in_=x_blocks[:, 2 * b : 2 * b + 2, c * K_PASS : (c + 1) * K_PASS],
-                )
+        def load_x_block(r):
+            x_rows = x_pool.tile([P, D_MODEL], BF16)
+            nc.sync.dma_start(
+                out=x_rows[:], in_=x_blocks[:, r : r + 1, :].rearrange("m o k -> m (o k)")
+            )
             return x_rows
 
         def load_w_chunk(g, c):
@@ -85,15 +87,15 @@ def tile_multiqueryattention_pa_kernel(tc, x, sin, cos, W_qkv, out_0, out_1, out
         sin_raw = const.tile([P, TOKEN_BLOCKS, HEAD_DIM], BF16)
 
         w_raw_of = {}
-        x_rows_of = []
-        for c in range(PASSES):
-            w_raw_of[(0, c)] = load_w_chunk(0, c)
-            x_rows_of.append(load_x_chunk(c))
-        nc.sync.dma_start(out=cos_raw[:], in_=cos_blocks)
-        nc.sync.dma_start(out=sin_raw[:], in_=sin_blocks)
-        for g in range(1, len(groups)):
-            for c in range(PASSES):
-                w_raw_of[(g, c)] = load_w_chunk(g, c)
+        x_rows_of = {}
+        for kind, index in arrivals:
+            if kind == "w":
+                w_raw_of[index] = load_w_chunk(*chunks[index])
+                if index == PASSES - 1:
+                    nc.sync.dma_start(out=cos_raw[:], in_=cos_blocks)
+                    nc.sync.dma_start(out=sin_raw[:], in_=sin_blocks)
+            else:
+                x_rows_of[index] = load_x_block(index)
 
         identity = const.tile([P, P], F32)
         make_identity(nc, identity[:])
@@ -118,27 +120,27 @@ def tile_multiqueryattention_pa_kernel(tc, x, sin, cos, W_qkv, out_0, out_1, out
         make_tables(Q_SCALE, cos_q, sin_q)
         make_tables(1.0, cos_k, sin_k)
 
-        x_codes = const.tile([P, PASSES, TOKENS], U32, align_bytes=64)
-        x_scales = const.tile([P, PASSES, TOKENS], U8, align_bytes=64)
+        x_codes = const.tile([P, TOKEN_BLOCKS, PASSES * P], U32, align_bytes=64)
+        x_scales = const.tile([P, TOKEN_BLOCKS, PASSES * P], U8, align_bytes=64)
 
-        def transpose_x_chunk(c):
-            x_words = x_rows_of[c][:].bitcast(F32)
+        def transpose_x_block(r):
+            x_words = x_rows_of[r][:].bitcast(F32)
             x_banks = []
-            for b in range(TOKEN_BLOCKS // 2):
+            for b in range(PASSES // 2):
                 bank = psum_odd.tile([P, GROUP_COLS], F32, tag="bank")
                 for u in range(2):
-                    for rr in range(2):
-                        word = 2 * P * (2 * b + rr) + P * u
+                    for cc in range(2):
+                        word = 2 * P * (2 * b + cc) + P * u
                         nc.tensor.transpose(
-                            bank[:, (2 * u + rr) * P : (2 * u + rr + 1) * P],
+                            bank[:, (2 * u + cc) * P : (2 * u + cc + 1) * P],
                             x_words[:, word : word + P],
                             identity[:],
                         )
                 x_banks.append(bank)
             return x_banks
 
-        def collect_x_chunk(x_banks):
-            x_grouped = x_stage.tile([P, TOKENS * PACK], BF16, align_bytes=64)
+        def collect_x_block(x_banks):
+            x_grouped = x_stage.tile([P, PASSES * P * PACK], BF16, align_bytes=64)
             grouped_words = x_grouped[:].bitcast(F32).rearrange("p (n u) -> p n u", u=2)
             nc.vector.tensor_copy(
                 out=grouped_words[:, 0 : 2 * P, :],
@@ -150,16 +152,18 @@ def tile_multiqueryattention_pa_kernel(tc, x, sin, cos, W_qkv, out_0, out_1, out
             )
             return x_grouped
 
-        def quantise_x_chunk(c, x_grouped):
+        def quantise_x_block(r, x_grouped):
             nc.vector.quantize_mx(
-                out=x_codes[:, c, :].bitcast(FP8X4), scales=x_scales[:, c, :], in_=x_grouped[:]
+                out=x_codes[:, r, :].bitcast(FP8X4), scales=x_scales[:, r, :], in_=x_grouped[:]
             )
 
-        def regroup_w_chunk(g, c, vector_eighths):
+        def regroup_w_chunk(n):
+            g = chunks[n][0]
             width = groups[g][1]
+            vector_eighths = VECTOR_EIGHTHS_FIRST if n <= PASSES else VECTOR_EIGHTHS
             split = width - width * vector_eighths // 8
             w_grouped = grouped_pool.tile([P, width, PACK], BF16, align_bytes=64)
-            w_raw = w_raw_of[(g, c)]
+            w_raw = w_raw_of[n]
             nc.scalar.copy(
                 out=w_grouped[:, 0:split, :].rearrange("p (n i) t -> p n t i", i=RUN),
                 in_=w_raw[:, :, 0:split].rearrange("p t (n i) -> p n t i", i=RUN),
@@ -170,36 +174,43 @@ def tile_multiqueryattention_pa_kernel(tc, x, sin, cos, W_qkv, out_0, out_1, out
             )
             return w_grouped
 
-        def quantise_w_chunk(g, c, w_grouped, w_codes, w_scales):
+        w_codes_of = {}
+        w_scales_of = {}
+
+        def quantise_w_chunk(g, c, w_grouped):
             width = groups[g][1]
+            if c == 0:
+                w_codes_of[g] = codes_pool.tile(
+                    [P, PASSES, GROUP_COLS], U32, align_bytes=64, name="w_codes"
+                )
+                w_scales_of[g] = codes_pool.tile(
+                    [P, PASSES, GROUP_COLS], U8, align_bytes=64, name="w_scales"
+                )
             nc.vector.quantize_mx(
-                out=w_codes[:, c, 0:width].bitcast(FP8X4),
-                scales=w_scales[:, c, 0:width],
+                out=w_codes_of[g][:, c, 0:width].bitcast(FP8X4),
+                scales=w_scales_of[g][:, c, 0:width],
                 in_=w_grouped[:].rearrange("p n t -> p (n t)"),
             )
 
-        def open_group(g):
-            w_codes = codes_pool.tile([P, PASSES, GROUP_COLS], U32, align_bytes=64)
-            w_scales = codes_pool.tile([P, PASSES, GROUP_COLS], U8, align_bytes=64)
-            psum_half = psum_even if g % 2 == 0 else psum_odd
-            banks = [
-                psum_half.tile([P, GROUP_COLS], F32, tag="bank", name="acc")
-                for r in range(TOKEN_BLOCKS)
-            ]
-            return w_codes, w_scales, banks
+        bank_of = {}
+        complete = []
 
-        def multiply_chunk(g, c, w_codes, w_scales, banks):
+        def multiply(g, c, r):
             width = groups[g][1]
-            for r in range(TOKEN_BLOCKS):
-                nc.tensor.matmul_mx(
-                    out=banks[r][:, 0:width],
-                    lhsT=x_codes[:, c, r * P : (r + 1) * P].bitcast(FP8X4),
-                    lhsT_scale=x_scales[:, c, r * P : (r + 1) * P],
-                    rhs=w_codes[:, c, 0:width].bitcast(FP8X4),
-                    rhs_scale=w_scales[:, c, 0:width],
-                    start=(c == 0),
-                    stop=(c == PASSES - 1),
-                )
+            if c == 0:
+                psum_half = psum_even if g % 2 == 0 else psum_odd
+                bank_of[(g, r)] = psum_half.tile([P, GROUP_COLS], F32, tag="bank", name="acc")
+            nc.tensor.matmul_mx(
+                out=bank_of[(g, r)][:, 0:width],
+                lhsT=x_codes[:, r, c * P : (c + 1) * P].bitcast(FP8X4),
+                lhsT_scale=x_scales[:, r, c * P : (c + 1) * P],
+                rhs=w_codes_of[g][:, c, 0:width].bitcast(FP8X4),
+                rhs_scale=w_scales_of[g][:, c, 0:width],
+                start=(c == 0),
+                stop=(c == PASSES - 1),
+            )
+            if c == PASSES - 1:
+                complete.append((g, r))
 
         def rope(heads, u, cos_table, sin_table, rotated):
             direct = product_pool.tile([P, heads, HEAD_DIM], F32)
@@ -217,68 +228,74 @@ def tile_multiqueryattention_pa_kernel(tc, x, sin, cos, W_qkv, out_0, out_1, out
                 )
             nc.gpsimd.tensor_tensor(out=rotated, in0=direct[:], in1=crossed[:], op=ADD)
 
-        def finish_bank(g, r, bank, rotated, v_rows):
+        rotated_of = {}
+
+        def finish_bank(g, r):
             first, width = groups[g]
             is_q = first < Q_HEADS * HEAD_DIM
-            heads = rotated.shape[1]
+            heads = width // HEAD_DIM if is_q else 1
+            if r == 0:
+                rotated_of[g] = out_pool.tile(
+                    [P, heads, TOKEN_BLOCKS, HEAD_DIM], F32, tag="rotated", name="rotated"
+                )
+            rotated = rotated_of[g]
             rope(
                 heads,
-                bank[:, 0 : heads * HEAD_DIM].rearrange("p (h d) -> p h d", d=HEAD_DIM),
+                bank_of[(g, r)][:, 0 : heads * HEAD_DIM].rearrange("p (h d) -> p h d", d=HEAD_DIM),
                 (cos_q if is_q else cos_k)[:, r, :],
                 (sin_q if is_q else sin_k)[:, r, :],
                 rotated[:, :, r, :],
             )
-            if not is_q:
-                nc.vector.tensor_copy(out=v_rows[:, 0, r, :], in_=bank[:, HEAD_DIM : 2 * HEAD_DIM])
             if r == TOKEN_BLOCKS - 1:
-                if is_q:
-                    head = first // HEAD_DIM
-                    nc.sync.dma_start(
-                        out=q_view[:, head : head + heads, :],
-                        in_=rotated[:].rearrange("p h r d -> p h (r d)"),
-                    )
-                else:
-                    nc.sync.dma_start(out=v_view, in_=v_rows[:].rearrange("p h r d -> p h (r d)"))
-                    nc.sync.dma_start(out=k_view, in_=rotated[:].rearrange("p h r d -> p h (r d)"))
-
-        def open_outputs(g):
-            first, width = groups[g]
-            is_q = first < Q_HEADS * HEAD_DIM
-            heads = width // HEAD_DIM if is_q else 1
-            rotated = out_pool.tile([P, heads, TOKEN_BLOCKS, HEAD_DIM], F32, tag="rotated")
-            v_rows = None
-            if not is_q:
-                v_rows = out_pool.tile([P, 1, TOKEN_BLOCKS, HEAD_DIM], F32, tag="v_rows")
-            return rotated, v_rows
-
-        assert PASSES == TOKEN_BLOCKS
-        steps = len(groups) * PASSES
-        x_banks_of = [transpose_x_chunk(c) for c in range(X_AHEAD)]
-        w_grouped_next = regroup_w_chunk(0, 0, VECTOR_EIGHTHS_FIRST)
-        for n in range(steps):
-            g, c = divmod(n, PASSES)
-            w_grouped = w_grouped_next
-            if g == 0:
-                x_grouped = collect_x_chunk(x_banks_of[c])
-            if c == 0:
-                if g > 0:
-                    done_banks = banks
-                    rotated, v_rows = open_outputs(g - 1)
-                w_codes, w_scales, banks = open_group(g)
-            quantise_w_chunk(g, c, w_grouped, w_codes, w_scales)
-            if g == 0:
-                quantise_x_chunk(c, x_grouped)
-            multiply_chunk(g, c, w_codes, w_scales, banks)
-            if n + 1 < steps:
-                w_grouped_next = regroup_w_chunk(
-                    (n + 1) // PASSES,
-                    (n + 1) % PASSES,
-                    VECTOR_EIGHTHS_FIRST if g == 0 else VECTOR_EIGHTHS,
+                head = first // HEAD_DIM
+                nc.sync.dma_start(
+                    out=q_view[:, head : head + heads, :] if is_q else k_view,
+                    in_=rotated[:].rearrange("p h r d -> p h (r d)"),
                 )
-            if g == 0 and c + X_AHEAD < PASSES:
-                x_banks_of.append(transpose_x_chunk(c + X_AHEAD))
-            if g > 0:
-                finish_bank(g - 1, c, done_banks[c], rotated, v_rows)
-        rotated, v_rows = open_outputs(len(groups) - 1)
+
+        quantised = []
+        x_blocks_ready = 0
+        finished = 0
+        x_banks_of = {}
+        for kind, index in arrivals[0:X_AHEAD]:
+            if kind == "x":
+                x_banks_of[index] = transpose_x_block(index)
+        w_grouped_next = regroup_w_chunk(0)
+        for step, (kind, index) in enumerate(arrivals):
+            due = complete[finished : finished + 1]
+            finished += len(due)
+            following = arrivals[step + 1 : step + 2]
+            for next_kind, next_index in arrivals[step + X_AHEAD : step + X_AHEAD + 1]:
+                if next_kind == "x":
+                    x_banks_of[next_index] = transpose_x_block(next_index)
+            if kind == "x":
+                x_grouped = collect_x_block(x_banks_of[index])
+                for g, r in due:
+                    finish_bank(g, r)
+            else:
+                g, c = chunks[index]
+                quantise_w_chunk(g, c, w_grouped_next)
+                quantised.append((g, c))
+                for r in range(x_blocks_ready):
+                    multiply(g, c, r)
+            for next_kind, next_index in following:
+                if next_kind == "w":
+                    w_grouped_next = regroup_w_chunk(next_index)
+            if kind == "x":
+                quantise_x_block(index, x_grouped)
+                for g, c in quantised:
+                    multiply(g, c, index)
+                x_blocks_ready += 1
+            else:
+                for g, r in due:
+                    finish_bank(g, r)
+        for g, r in complete[finished:]:
+            finish_bank(g, r)
+
+        v_rows = out_pool.tile([P, 1, TOKEN_BLOCKS, HEAD_DIM], F32)
         for r in range(TOKEN_BLOCKS):
-            finish_bank(len(groups) - 1, r, banks[r], rotated, v_rows)
+            nc.vector.tensor_copy(
+                out=v_rows[:, 0, r, :],
+                in_=bank_of[(len(groups) - 1, r)][:, HEAD_DIM : 2 * HEAD_DIM],
+            )
+        nc.sync.dma_start(out=v_view, in_=v_rows[:].rearrange("p h r d -> p h (r d)"))

from contextlib import ExitStack

import concourse.mybir as mybir
from concourse.masks import make_identity

F32 = mybir.dt.float32
BF16 = mybir.dt.bfloat16
U32 = mybir.dt.uint32
U8 = mybir.dt.uint8
FP8X4 = mybir.dt.float8_e4m3fn_x4
MULT = mybir.AluOpType.mult
ADD = mybir.AluOpType.add

P = 128
PACK = 4
K_PASS = P * PACK
TOKENS = 512
D_MODEL = 2048
HEAD_DIM = 128
HALF = HEAD_DIM // 2
Q_HEADS = 16
N_COLS = (Q_HEADS + 2) * HEAD_DIM
PASSES = D_MODEL // K_PASS
TOKEN_BLOCKS = TOKENS // P
GROUP_COLS = 512
Q_SCALE = HEAD_DIM**-0.5
RUN = 4
PSUM_BANKS = 8
X_AHEAD = 2
VECTOR_EIGHTHS_FIRST = 3
VECTOR_EIGHTHS = 1

FLOPS = 2 * TOKENS * D_MODEL * N_COLS


def tile_multiqueryattention_pa_kernel(tc, x, sin, cos, W_qkv, out_0, out_1, out_2):
    nc = tc.nc
    groups = [(first, min(GROUP_COLS, N_COLS - first)) for first in range(0, N_COLS, GROUP_COLS)]
    chunks = [(g, c) for g in range(len(groups)) for c in range(PASSES)]
    arrivals = []
    for n in range(len(chunks)):
        arrivals.append(("w", n))
        if n < TOKEN_BLOCKS:
            arrivals.append(("x", n))

    x_blocks = x.rearrange("b (m r) k -> (b m) r k", r=TOKEN_BLOCKS)
    cos_blocks = cos.rearrange("(m r) d -> m r d", r=TOKEN_BLOCKS)
    sin_blocks = sin.rearrange("(m r) d -> m r d", r=TOKEN_BLOCKS)
    q_view = out_0.rearrange("b h (m r) d -> m (b h) (r d)", r=TOKEN_BLOCKS)
    k_view = out_1.rearrange("b (m r) d -> m b (r d)", r=TOKEN_BLOCKS)
    v_view = out_2.rearrange("b (m r) d -> m b (r d)", r=TOKEN_BLOCKS)

    with ExitStack() as ctx:
        const = ctx.enter_context(tc.tile_pool(name="const", bufs=1))
        x_pool = ctx.enter_context(tc.tile_pool(name="x_pool", bufs=TOKEN_BLOCKS))
        x_stage = ctx.enter_context(tc.tile_pool(name="x_stage", bufs=2))
        raw_pool = ctx.enter_context(tc.tile_pool(name="raw_pool", bufs=len(chunks)))
        grouped_pool = ctx.enter_context(tc.tile_pool(name="grouped_pool", bufs=4))
        codes_pool = ctx.enter_context(tc.tile_pool(name="codes_pool", bufs=3))
        product_pool = ctx.enter_context(tc.tile_pool(name="product_pool", bufs=4))
        out_pool = ctx.enter_context(tc.tile_pool(name="out_pool", bufs=3))
        psum_even = ctx.enter_context(tc.psum_pool(name="psum_even", bufs=PSUM_BANKS // 2))
        psum_odd = ctx.enter_context(tc.psum_pool(name="psum_odd", bufs=PSUM_BANKS // 2))
        ctx.enter_context(tc.manual_schedule())

        def load_x_block(r):
            x_rows = x_pool.tile([P, D_MODEL], BF16)
            nc.sync.dma_start(
                out=x_rows[:], in_=x_blocks[:, r : r + 1, :].rearrange("m o k -> m (o k)")
            )
            return x_rows

        def load_w_chunk(g, c):
            first, width = groups[g]
            w_raw = raw_pool.tile([P, PACK, width], BF16)
            for u in range(2):
                row = K_PASS * c + 2 * P * u
                nc.sync.dma_start(
                    out=w_raw[:, 2 * u : 2 * u + 2, :],
                    in_=W_qkv[row : row + 2 * P, first : first + width].rearrange(
                        "(p e) w -> p e w", e=2
                    ),
                )
            return w_raw

        cos_raw = const.tile([P, TOKEN_BLOCKS, HEAD_DIM], BF16)
        sin_raw = const.tile([P, TOKEN_BLOCKS, HEAD_DIM], BF16)

        w_raw_of = {}
        x_rows_of = {}
        for kind, index in arrivals:
            if kind == "w":
                w_raw_of[index] = load_w_chunk(*chunks[index])
                if index == PASSES - 1:
                    nc.sync.dma_start(out=cos_raw[:], in_=cos_blocks)
                    nc.sync.dma_start(out=sin_raw[:], in_=sin_blocks)
            else:
                x_rows_of[index] = load_x_block(index)

        identity = const.tile([P, P], F32)
        make_identity(nc, identity[:])

        def make_tables(factor, cos_table, sin_table):
            nc.gpsimd.tensor_scalar(
                out=cos_table[:], in0=cos_raw[:], scalar1=factor, scalar2=0.0, op0=MULT, op1=ADD
            )
            nc.gpsimd.tensor_scalar(
                out=sin_table[:, :, 0:HALF], in0=sin_raw[:, :, 0:HALF],
                scalar1=-factor, scalar2=0.0, op0=MULT, op1=ADD,
            )
            nc.gpsimd.tensor_scalar(
                out=sin_table[:, :, HALF:HEAD_DIM], in0=sin_raw[:, :, HALF:HEAD_DIM],
                scalar1=factor, scalar2=0.0, op0=MULT, op1=ADD,
            )

        cos_q = const.tile([P, TOKEN_BLOCKS, HEAD_DIM], F32)
        sin_q = const.tile([P, TOKEN_BLOCKS, HEAD_DIM], F32)
        cos_k = const.tile([P, TOKEN_BLOCKS, HEAD_DIM], F32)
        sin_k = const.tile([P, TOKEN_BLOCKS, HEAD_DIM], F32)
        make_tables(Q_SCALE, cos_q, sin_q)
        make_tables(1.0, cos_k, sin_k)

        x_codes = const.tile([P, TOKEN_BLOCKS, PASSES * P], U32, align_bytes=64)
        x_scales = const.tile([P, TOKEN_BLOCKS, PASSES * P], U8, align_bytes=64)

        def transpose_x_block(r):
            x_words = x_rows_of[r][:].bitcast(F32)
            x_banks = []
            for b in range(PASSES // 2):
                bank = psum_odd.tile([P, GROUP_COLS], F32, tag="bank")
                for u in range(2):
                    for cc in range(2):
                        word = 2 * P * (2 * b + cc) + P * u
                        nc.tensor.transpose(
                            bank[:, (2 * u + cc) * P : (2 * u + cc + 1) * P],
                            x_words[:, word : word + P],
                            identity[:],
                        )
                x_banks.append(bank)
            return x_banks

        def collect_x_block(x_banks):
            x_grouped = x_stage.tile([P, PASSES * P * PACK], BF16, align_bytes=64)
            grouped_words = x_grouped[:].bitcast(F32).rearrange("p (n u) -> p n u", u=2)
            nc.vector.tensor_copy(
                out=grouped_words[:, 0 : 2 * P, :],
                in_=x_banks[0][:].rearrange("p (u n) -> p n u", u=2),
            )
            nc.scalar.copy(
                out=grouped_words[:, 2 * P : 4 * P, :],
                in_=x_banks[1][:].rearrange("p (u n) -> p n u", u=2),
            )
            return x_grouped

        def quantise_x_block(r, x_grouped):
            nc.vector.quantize_mx(
                out=x_codes[:, r, :].bitcast(FP8X4), scales=x_scales[:, r, :], in_=x_grouped[:]
            )

        def regroup_w_chunk(n):
            g = chunks[n][0]
            width = groups[g][1]
            vector_eighths = VECTOR_EIGHTHS_FIRST if n <= PASSES else VECTOR_EIGHTHS
            split = width - width * vector_eighths // 8
            w_grouped = grouped_pool.tile([P, width, PACK], BF16, align_bytes=64)
            w_raw = w_raw_of[n]
            nc.scalar.copy(
                out=w_grouped[:, 0:split, :].rearrange("p (n i) t -> p n t i", i=RUN),
                in_=w_raw[:, :, 0:split].rearrange("p t (n i) -> p n t i", i=RUN),
            )
            nc.vector.tensor_copy(
                out=w_grouped[:, split:width, :].rearrange("p (n i) t -> p n t i", i=RUN),
                in_=w_raw[:, :, split:width].rearrange("p t (n i) -> p n t i", i=RUN),
            )
            return w_grouped

        w_codes_of = {}
        w_scales_of = {}

        def quantise_w_chunk(g, c, w_grouped):
            width = groups[g][1]
            if c == 0:
                w_codes_of[g] = codes_pool.tile(
                    [P, PASSES, GROUP_COLS], U32, align_bytes=64, name="w_codes"
                )
                w_scales_of[g] = codes_pool.tile(
                    [P, PASSES, GROUP_COLS], U8, align_bytes=64, name="w_scales"
                )
            nc.vector.quantize_mx(
                out=w_codes_of[g][:, c, 0:width].bitcast(FP8X4),
                scales=w_scales_of[g][:, c, 0:width],
                in_=w_grouped[:].rearrange("p n t -> p (n t)"),
            )

        bank_of = {}
        complete = []

        def multiply(g, c, r):
            width = groups[g][1]
            if c == 0:
                psum_half = psum_even if g % 2 == 0 else psum_odd
                bank_of[(g, r)] = psum_half.tile([P, GROUP_COLS], F32, tag="bank", name="acc")
            nc.tensor.matmul_mx(
                out=bank_of[(g, r)][:, 0:width],
                lhsT=x_codes[:, r, c * P : (c + 1) * P].bitcast(FP8X4),
                lhsT_scale=x_scales[:, r, c * P : (c + 1) * P],
                rhs=w_codes_of[g][:, c, 0:width].bitcast(FP8X4),
                rhs_scale=w_scales_of[g][:, c, 0:width],
                start=(c == 0),
                stop=(c == PASSES - 1),
            )
            if c == PASSES - 1:
                complete.append((g, r))

        def rope(heads, u, cos_table, sin_table, rotated):
            direct = product_pool.tile([P, heads, HEAD_DIM], F32)
            crossed = product_pool.tile([P, heads, HEAD_DIM], F32)
            nc.vector.tensor_tensor(
                out=direct[:], in0=u,
                in1=cos_table.unsqueeze(1).to_broadcast([P, heads, HEAD_DIM]), op=MULT,
            )
            for half in range(2):
                here = slice(half * HALF, (half + 1) * HALF)
                other = slice((1 - half) * HALF, (2 - half) * HALF)
                nc.vector.tensor_tensor(
                    out=crossed[:, :, here], in0=u[:, :, other],
                    in1=sin_table[:, here].unsqueeze(1).to_broadcast([P, heads, HALF]), op=MULT,
                )
            nc.gpsimd.tensor_tensor(out=rotated, in0=direct[:], in1=crossed[:], op=ADD)

        rotated_of = {}

        def finish_bank(g, r):
            first, width = groups[g]
            is_q = first < Q_HEADS * HEAD_DIM
            heads = width // HEAD_DIM if is_q else 1
            if r == 0:
                rotated_of[g] = out_pool.tile(
                    [P, heads, TOKEN_BLOCKS, HEAD_DIM], F32, tag="rotated", name="rotated"
                )
            rotated = rotated_of[g]
            rope(
                heads,
                bank_of[(g, r)][:, 0 : heads * HEAD_DIM].rearrange("p (h d) -> p h d", d=HEAD_DIM),
                (cos_q if is_q else cos_k)[:, r, :],
                (sin_q if is_q else sin_k)[:, r, :],
                rotated[:, :, r, :],
            )
            if r == TOKEN_BLOCKS - 1:
                head = first // HEAD_DIM
                nc.sync.dma_start(
                    out=q_view[:, head : head + heads, :] if is_q else k_view,
                    in_=rotated[:].rearrange("p h r d -> p h (r d)"),
                )

        quantised = []
        x_blocks_ready = 0
        finished = 0
        x_banks_of = {}
        for kind, index in arrivals[0:X_AHEAD]:
            if kind == "x":
                x_banks_of[index] = transpose_x_block(index)
        w_grouped_next = regroup_w_chunk(0)
        for step, (kind, index) in enumerate(arrivals):
            due = complete[finished : finished + 1]
            finished += len(due)
            following = arrivals[step + 1 : step + 2]
            for next_kind, next_index in arrivals[step + X_AHEAD : step + X_AHEAD + 1]:
                if next_kind == "x":
                    x_banks_of[next_index] = transpose_x_block(next_index)
            if kind == "x":
                x_grouped = collect_x_block(x_banks_of[index])
                for g, r in due:
                    finish_bank(g, r)
            else:
                g, c = chunks[index]
                quantise_w_chunk(g, c, w_grouped_next)
                quantised.append((g, c))
                for r in range(x_blocks_ready):
                    multiply(g, c, r)
            for next_kind, next_index in following:
                if next_kind == "w":
                    w_grouped_next = regroup_w_chunk(next_index)
            if kind == "x":
                quantise_x_block(index, x_grouped)
                for g, c in quantised:
                    multiply(g, c, index)
                x_blocks_ready += 1
            else:
                for g, r in due:
                    finish_bank(g, r)
        for g, r in complete[finished:]:
            finish_bank(g, r)

        v_rows = out_pool.tile([P, 1, TOKEN_BLOCKS, HEAD_DIM], F32)
        for r in range(TOKEN_BLOCKS):
            nc.vector.tensor_copy(
                out=v_rows[:, 0, r, :],
                in_=bank_of[(len(groups) - 1, r)][:, HEAD_DIM : 2 * HEAD_DIM],
            )
        nc.sync.dma_start(out=v_view, in_=v_rows[:].rearrange("p h r d -> p h (r d)"))
